import numpy as np
import ml_dtypes


def mxq(x, axis, fmt="e4m3"):
    dtype, down = {"e4m3": (ml_dtypes.float8_e4m3fn, 7), "e5m2": (ml_dtypes.float8_e5m2, 14)}[fmt]
    v = np.moveaxis(np.asarray(x, np.float32).astype(ml_dtypes.bfloat16).astype(np.float64), axis, -1)
    blocks = v.reshape(v.shape[:-1] + (-1, 32))
    amax = np.abs(blocks).max(-1, keepdims=True)
    byte = np.maximum(np.where(amax > 0, np.frexp(amax)[1] - 1 + 127, 0) - down, 1)
    scale = np.exp2(byte - 127.0)
    codes = (blocks / scale).astype(np.float32).astype(dtype).astype(np.float64)
    return np.moveaxis((codes * scale).reshape(v.shape), -1, axis)


WIDE = False


def mx_kscale(k):
    if not WIDE:
        return np.ones(k)
    levels = np.array([10, -10, 5, -5, 0])
    if k % 512:
        return np.exp2(np.random.permutation(np.resize(levels, k // 32))).repeat(32)
    a = np.empty((k // 512, 16))
    for p in range(k // 512):
        a[p, :8] = np.random.permutation(np.resize(levels, 8))
        for g in range(8):
            far = levels[np.abs(levels - a[p, g]) >= 10]
            a[p, g + 8] = far[np.random.randint(len(far))]
    return np.exp2(a.ravel()).repeat(32)


BF16 = ml_dtypes.bfloat16


def bf(x):
    return np.asarray(x, np.float32).astype(BF16)


def f64(x):
    return np.asarray(x).astype(np.float64)


N, D_FEAT, D_EMB, H = 4, 511, 512, 4
SEQ = D_FEAT + 1
EPS = 1e-5


def ln(x):
    m = x.mean(-1, keepdims=True)
    v = ((x - m) ** 2).mean(-1, keepdims=True)
    return (x - m) / np.sqrt(v + EPS)


def setup_inputs():
    s = mx_kscale(D_EMB)
    return {'Z': bf(0.5 + 1.5 * np.random.standard_normal((N, D_FEAT))),
            'feat_emb': bf(np.random.standard_normal((D_FEAT, D_EMB)) * 0.02 + 0.01),
            'label_token': bf(np.random.standard_normal((1, 1, D_EMB)) * 0.02 + 0.01),
            'g1': bf((1.0 + 0.1 * np.random.standard_normal(D_EMB)) * s),
            'be1': bf(0.1 * np.random.standard_normal(D_EMB) * s),
            'wk': bf(np.random.standard_normal((D_EMB, D_EMB)) / np.sqrt(D_EMB) / s[:, None]),
            'bk': bf(0.3 * np.random.standard_normal(D_EMB)),
            'wv': bf(np.random.standard_normal((D_EMB, D_EMB)) / np.sqrt(D_EMB) / s[:, None]),
            'bv': bf(0.3 * np.random.standard_normal(D_EMB))}


def reference(Z, feat_emb, label_token, g1, be1, wk, bk, wv, bv):
    n = Z.shape[0]
    zn = ln(f64(Z))
    x_feats = zn[..., None] * f64(feat_emb)[None]
    lab = np.broadcast_to(f64(label_token), (n, 1, D_EMB))
    x = np.concatenate([x_feats, lab], axis=1)
    xn = ln(x) * f64(g1) + f64(be1)
    xq = mxq(xn, 2, 'e4m3')
    k = (xq @ mxq(f64(wk), 0, 'e4m3')) + f64(bk)
    v = (xq @ mxq(f64(wv), 0, 'e4m3')) + f64(bv)
    return k, v

@@ -1,0 +1,317 @@
+from contextlib import ExitStack
+
+import concourse.mybir as mybir
+from concourse.masks import make_identity
+
+F32 = mybir.dt.float32
+BF16 = mybir.dt.bfloat16
+U32 = mybir.dt.uint32
+U8 = mybir.dt.uint8
+FP8X4 = mybir.dt.float8_e4m3fn_x4
+ALU = mybir.AluOpType
+ACT = mybir.ActivationFunctionType
+
+P = 128
+PACK = 4
+BATCH = 4
+D_FEAT = 511
+SEQ = D_FEAT + 1
+D_EMB = 512
+D_OUT = 512
+BLOCKS = SEQ // P
+EPS = 1e-5
+
+UNITS = BLOCKS * BATCH
+PAIR = 2
+PAIRS = UNITS // PAIR
+PAIR_BANKS = 2 * PAIR
+VECTOR_UNITS = BATCH
+TURN_AHEAD = 2
+FORM_AHEAD = 4
+HELP_FROM = PAIRS - FORM_AHEAD + 1
+
+FLOPS = 2 * BATCH * SEQ * D_EMB * 2 * D_OUT
+
+
+def tile_causalfeaturetransformer_pa_kernel(
+    tc, Z, feat_emb, label_token, g1, be1, wk, bk, wv, bv, out_0, out_1
+):
+    nc = tc.nc
+    weights = (wk, wv)
+    outs = (out_0, out_1)
+
+    with ExitStack() as ctx:
+        keep = ctx.enter_context(tc.tile_pool(name="keep", bufs=1))
+        turned_banks = ctx.enter_context(tc.psum_pool(name="turned_banks", bufs=2))
+        acc_banks = ctx.enter_context(tc.psum_pool(name="acc_banks", bufs=6))
+        ctx.enter_context(tc.manual_schedule())
+
+        ident = keep.tile([P, P], F32)
+        ident_bf = keep.tile([P, P], BF16)
+        warm = keep.tile([P, 1], F32)
+        z_rows = keep.tile([P, SEQ], BF16)
+        norm_rows = keep.tile([P, D_EMB], BF16)
+        bias_rows = keep.tile([P, D_OUT], BF16)
+        emb = keep.tile([P, BLOCKS, D_EMB], BF16)
+        z_stats = keep.tile([P, 6], F32)
+        z_mv = keep.tile([P, 2], F32)
+        z_var_eps = keep.tile([P, 1], F32)
+        z_terms = keep.tile([P, P + SEQ], F32)
+        e_stats = keep.tile([P, BLOCKS, 6], F32)
+        e_mv = keep.tile([P, BLOCKS, 2], F32)
+        shaped = keep.tile([P, BLOCKS, D_EMB], F32)
+        root = keep.tile([P, BLOCKS, 2 * BATCH], F32)
+        slope = keep.tile([P, BLOCKS, BATCH], F32)
+        be1_all = keep.tile([P, D_EMB], BF16)
+        bias_all = [keep.tile([P, D_OUT], BF16, name="bias_all%d" % w) for w in range(2)]
+        w_raw = [keep.tile([P, PACK, D_OUT], BF16, name="w_raw%d" % w) for w in range(2)]
+        w_grouped = [
+            keep.tile([P, D_OUT, PACK], BF16, name="w_grouped%d" % w, align_bytes=64) for w in range(2)
+        ]
+        w_codes = [keep.tile([P, D_OUT], U32, name="w_codes%d" % w, align_bytes=64) for w in range(2)]
+        w_scales = [keep.tile([P, D_OUT], U8, name="w_scales%d" % w, align_bytes=64) for w in range(2)]
+        scaled = {u: keep.tile([P, D_EMB], F32, name="scaled%d" % u) for u in range(VECTOR_UNITS, UNITS)}
+        xn = [keep.tile([P, D_EMB], BF16, name="xn%d" % u) for u in range(UNITS)]
+        x_grouped = [
+            keep.tile([P, PAIR, P, PACK], BF16, name="x_grouped%d" % c, align_bytes=64)
+            for c in range(PAIRS)
+        ]
+        x_codes = [keep.tile([P, PAIR * P], U32, name="x_codes%d" % c, align_bytes=64) for c in range(PAIRS)]
+        x_scales = [keep.tile([P, PAIR * P], U8, name="x_scales%d" % c, align_bytes=64) for c in range(PAIRS)]
+        result = [keep.tile([P, D_OUT], F32, name="result%d" % b) for b in range(2 * UNITS)]
+        unbiased = {c: keep.tile([P, D_OUT], F32, name="unbiased%d" % c) for c in range(HELP_FROM, PAIRS)}
+
+        def by_slot(x):
+            return x.rearrange("q (p t) -> q t p", t=PACK)
+
+        def as_they_lie(x):
+            return x.rearrange("q (t p) -> q t p", t=PACK)
+
+        def spread_row(rows, r, view):
+            bank = acc_banks.tile([P, D_EMB], F32, name="acc")
+            nc.tensor.matmul(
+                out=bank[:].rearrange("q (t p) -> q t p", t=PACK),
+                lhsT=ident_bf[:, r : r + 1].to_broadcast([P, P]),
+                rhs=view(rows[:]),
+                start=True,
+                stop=True,
+            )
+            return bank
+
+        def turn_z_terms(first, end):
+            bank = turned_banks.tile([P, BLOCKS, P], F32, name="turned")
+            nc.tensor.transpose(bank[:, 0, :], z_terms[:, 0:P], ident[:])
+            for j in range(first, end):
+                nc.tensor.transpose(bank[:, 1 + j - first, :], z_terms[:, (1 + j) * P : (2 + j) * P], ident[:])
+            return bank
+
+        def measure(j):
+            nc.vector.bn_stats(out=e_stats[:, j, :], in_=emb[:, j, :])
+            nc.vector.bn_aggr(out=e_mv[:, j, :], in_=e_stats[:, j, :])
+
+        def shape(j):
+            nc.vector.scalar_tensor_tensor(
+                out=shaped[:, j, :].rearrange("q (t p) -> q t p", t=PACK),
+                in0=by_slot(emb[:, j, :]),
+                scalar=e_mv[:, j, 0:1],
+                in1=g1_bank[:].rearrange("q (t p) -> q t p", t=PACK),
+                op0=ALU.subtract,
+                op1=ALU.mult,
+            )
+
+        def slope_root(first, end, bank):
+            some = [P, end - first, BATCH]
+            d = bank[:, 1 : 1 + end - first, 0:BATCH]
+            part = root[:, first:end, 0:BATCH]
+            nc.vector.tensor_mul(out=part, in0=d, in1=e_mv[:, first:end, 1:2].to_broadcast(some))
+            nc.vector.tensor_mul(out=part, in0=d, in1=part)
+            nc.vector.tensor_add(out=part, in0=bank[:, 0:1, 0:BATCH].to_broadcast(some), in1=part)
+            nc.scalar.activation(out=part, in_=part, func=ACT.Sqrt)
+
+        def slope_divide(first, end, bank):
+            part = root[:, first:end, 0:BATCH]
+            nc.vector.reciprocal(out=part, in_=part)
+            nc.vector.tensor_mul(out=slope[:, first:end, :], in0=bank[:, 1 : 1 + end - first, 0:BATCH], in1=part)
+
+        def regroup_weight(w):
+            nc.gpsimd.tensor_scalar(
+                out=w_grouped[w][:],
+                in0=w_raw[w][:].rearrange("p t n -> p n t"),
+                scalar1=1.0,
+                scalar2=0.0,
+                op0=ALU.mult,
+                op1=ALU.add,
+            )
+
+        def quantise_weight(w):
+            nc.vector.quantize_mx(
+                out=w_codes[w][:].bitcast(FP8X4),
+                scales=w_scales[w][:],
+                in_=w_grouped[w][:].rearrange("p n t -> p (n t)"),
+            )
+
+        def form_on_vector(u):
+            j, n = divmod(u, BATCH)
+            nc.vector.scalar_tensor_tensor(
+                out=xn[u][:],
+                in0=shaped[:, j, :],
+                scalar=slope[:, j, n : n + 1],
+                in1=be1_bank[:],
+                op0=ALU.mult,
+                op1=ALU.add,
+            )
+
+        def form_on_scalar_and_gpsimd(u):
+            j, n = divmod(u, BATCH)
+            nc.scalar.activation(
+                out=scaled[u][:], in_=shaped[:, j, :], func=ACT.Copy, scale=slope[:, j, n : n + 1]
+            )
+            nc.gpsimd.tensor_tensor(out=xn[u][:], in0=scaled[u][:], in1=be1_all[:], op=ALU.add)
+
+        def turn_and_regroup(c):
+            turned = turned_banks.tile([P, PAIR, PACK, P], BF16)
+            for h in range(PAIR):
+                for t in range(PACK):
+                    nc.tensor.transpose(
+                        turned[:, h, t, :], xn[PAIR * c + h][:, t * P : (t + 1) * P], ident_bf[:]
+                    )
+            nc.scalar.copy(out=x_grouped[c][:], in_=turned[:].rearrange("p h t r -> p h r t"))
+
+        def quantise(c):
+            nc.vector.quantize_mx(
+                out=x_codes[c][:].bitcast(FP8X4),
+                scales=x_scales[c][:],
+                in_=x_grouped[c][:].rearrange("p h r t -> p (h r t)"),
+            )
+
+        def multiply(c):
+            banks = []
+            for h in range(PAIR):
+                tokens = slice(h * P, (h + 1) * P)
+                for w in range(2):
+                    acc = acc_banks.tile([P, D_OUT], F32)
+                    nc.tensor.matmul_mx(
+                        out=acc[:],
+                        lhsT=x_codes[c][:, tokens].bitcast(FP8X4),
+                        lhsT_scale=x_scales[c][:, tokens],
+                        rhs=w_codes[w][:].bitcast(FP8X4),
+                        rhs_scale=w_scales[w][:],
+                        start=True,
+                        stop=True,
+                    )
+                    banks.append(acc)
+            return banks
+
+        def add_bias_on_vector(c, b, banks):
+            nc.vector.tensor_add(out=result[PAIR_BANKS * c + b][:], in0=banks[b][:], in1=bias_all[b % 2][:])
+
+        def add_bias_on_scalar_and_gpsimd(c, b, banks):
+            nc.scalar.copy(out=unbiased[c][:], in_=banks[b][:])
+            nc.gpsimd.tensor_tensor(
+                out=result[PAIR_BANKS * c + b][:], in0=unbiased[c][:], in1=bias_all[b % 2][:], op=ALU.add
+            )
+
+        def store(c, b):
+            j, n = divmod(PAIR * c + b // 2, BATCH)
+            nc.sync.dma_start(out=outs[b % 2][n, j * P : (j + 1) * P, :], in_=result[PAIR_BANKS * c + b][:])
+
+        def load_row(rows, r, vector):
+            nc.sync.dma_start(out=rows[r : r + 1, :], in_=vector.rearrange("(a k) -> a k", a=1))
+
+        def load_weight(w):
+            nc.sync.dma_start(out=w_raw[w][:], in_=weights[w].rearrange("(p t) n -> p t n", p=P))
+
+        nc.vector.memset(norm_rows[:], 0.0)
+        nc.vector.memset(bias_rows[:], 0.0)
+        nc.sync.dma_start(out=z_rows[0:BATCH, 0:D_FEAT], in_=Z)
+        nc.sync.dma_start(out=emb[:, 0, :], in_=feat_emb[0:P, :])
+        load_row(norm_rows, 0, g1)
+        load_row(norm_rows, 1, be1)
+        nc.sync.dma_start(out=emb[:, 1, :], in_=feat_emb[P : 2 * P, :])
+        nc.sync.dma_start(out=emb[:, 2, :], in_=feat_emb[2 * P : 3 * P, :])
+        load_weight(0)
+        load_weight(1)
+        load_row(bias_rows, 0, bk)
+        load_row(bias_rows, 1, bv)
+        last = (BLOCKS - 1) * P
+        nc.sync.dma_start(out=emb[0:112, BLOCKS - 1, :], in_=feat_emb[last : last + 112, :])
+        nc.sync.dma_start(out=emb[112:127, BLOCKS - 1, :], in_=feat_emb[last + 112 : D_FEAT, :])
+        nc.sync.dma_start(
+            out=emb[127:128, BLOCKS - 1, :], in_=label_token.rearrange("a b k -> (a b) k")
+        )
+
+        make_identity(nc, ident[:])
+        nc.gpsimd.memset(z_terms[:], 0.0)
+        nc.vector.memset(warm[:], 1.0)
+        nc.scalar.activation(out=warm[:], in_=warm[:], func=ACT.Sqrt)
+        nc.vector.tensor_copy(out=ident_bf[:], in_=ident[:])
+
+        rows4 = slice(0, BATCH)
+        nc.vector.bn_stats(out=z_stats[rows4, :], in_=z_rows[rows4, 0:D_FEAT])
+        nc.vector.bn_aggr(out=z_mv[rows4, :], in_=z_stats[rows4, :])
+        nc.vector.tensor_scalar_sub(
+            out=z_terms[rows4, P : P + D_FEAT], in0=z_rows[rows4, 0:D_FEAT], scalar1=z_mv[rows4, 0:1]
+        )
+        nc.vector.tensor_scalar(
+            out=z_terms[rows4, 0:P],
+            in0=z_mv[rows4, 1:2].to_broadcast([BATCH, P]),
+            scalar1=EPS,
+            scalar2=EPS,
+            op0=ALU.add,
+            op1=ALU.mult,
+        )
+        nc.vector.tensor_scalar_add(out=z_var_eps[rows4, :], in0=z_mv[rows4, 1:2], scalar1=EPS)
+        g1_bank = spread_row(norm_rows, 0, by_slot)
+        be1_bank = spread_row(norm_rows, 1, by_slot)
+        nc.scalar.copy(out=be1_all[:], in_=be1_bank[:])
+        nc.scalar.activation(
+            out=z_terms[rows4, P + D_FEAT : P + SEQ], in_=z_var_eps[rows4, :], func=ACT.Sqrt
+        )
+        regroup_weight(0)
+        regroup_weight(1)
+        early = BLOCKS // 2
+        early_bank = turn_z_terms(0, early)
+        late_bank = turn_z_terms(early, BLOCKS)
+        for j in range(early):
+            measure(j)
+        slope_root(0, early, early_bank)
+        shape(0)
+        shape(1)
+        slope_divide(0, early, early_bank)
+        for u in range(VECTOR_UNITS, 2 * VECTOR_UNITS):
+            form_on_scalar_and_gpsimd(u)
+        form_on_vector(0)
+        form_on_vector(1)
+        for j in range(early, BLOCKS):
+            measure(j)
+        slope_root(early, BLOCKS, late_bank)
+        turn_and_regroup(0)
+        for w in range(2):
+            nc.scalar.copy(out=bias_all[w][:], in_=spread_row(bias_rows, w, as_they_lie)[:])
+        form_on_vector(2)
+        form_on_vector(3)
+        shape(2)
+        slope_divide(early, BLOCKS, late_bank)
+        turn_and_regroup(1)
+        quantise_weight(0)
+        quantise_weight(1)
+        quantise(0)
+        shape(3)
+
+        for step in range(PAIRS):
+            banks = multiply(step)
+            if step + FORM_AHEAD < PAIRS:
+                for h in range(PAIR):
+                    form_on_scalar_and_gpsimd(PAIR * (step + FORM_AHEAD) + h)
+            helped = step >= HELP_FROM
+            if helped:
+                add_bias_on_scalar_and_gpsimd(step, 0, banks)
+            if step + TURN_AHEAD < PAIRS:
+                turn_and_regroup(step + TURN_AHEAD)
+            for b in range(1 if helped else 0, PAIR_BANKS):
+                if b == 1 and step + 1 < PAIRS:
+                    quantise(step + 1)
+                add_bias_on_vector(step, b, banks)
+                store(step, b)
+                if helped and b == PAIR_BANKS // 2:
+                    store(step, 0)

@@ -7,6 +7,7 @@ F32 = mybir.dt.float32
 BF16 = mybir.dt.bfloat16
 U32 = mybir.dt.uint32
 U8 = mybir.dt.uint8
+I32 = mybir.dt.int32
 FP8X4 = mybir.dt.float8_e4m3fn_x4
 ALU = mybir.AluOpType
 ACT = mybir.ActivationFunctionType
@@ -28,7 +29,7 @@ PAIR_BANKS = 2 * PAIR
 VECTOR_UNITS = BATCH
 TURN_AHEAD = 2
 FORM_AHEAD = 4
-HELP_FROM = PAIRS - FORM_AHEAD + 1
+HELP_FROM = PAIRS - FORM_AHEAD - 1
 
 FLOPS = 2 * BATCH * SEQ * D_EMB * 2 * D_OUT
 
@@ -38,6 +39,7 @@ def tile_causalfeaturetransformer_pa_kernel(
 ):
     nc = tc.nc
     weights = (wk, wv)
+    biases = (bk, bv)
     outs = (out_0, out_1)
 
     with ExitStack() as ctx:
@@ -51,14 +53,17 @@ def tile_causalfeaturetransformer_pa_kernel(
         warm = keep.tile([P, 1], F32)
         z_rows = keep.tile([P, SEQ], BF16)
         norm_rows = keep.tile([P, D_EMB], BF16)
-        bias_rows = keep.tile([P, D_OUT], BF16)
         emb = keep.tile([P, BLOCKS, D_EMB], BF16)
         z_stats = keep.tile([P, 6], F32)
         z_mv = keep.tile([P, 2], F32)
-        z_var_eps = keep.tile([P, 1], F32)
-        z_terms = keep.tile([P, P + SEQ], F32)
-        e_stats = keep.tile([P, BLOCKS, 6], F32)
+        z_rstd = keep.tile([P, 1], F32)
+        f_rows = keep.tile([P, SEQ], F32)
+        f = keep.tile([P, BLOCKS, BATCH], F32)
+        f_squared = keep.tile([P, BLOCKS, BATCH], F32)
+        e_stats = keep.tile([P, 6], F32)
         e_mv = keep.tile([P, BLOCKS, 2], F32)
+        e_squares = keep.tile([P, BLOCKS], F32)
+        unused = keep.tile([P, D_EMB], BF16)
         shaped = keep.tile([P, BLOCKS, D_EMB], F32)
         root = keep.tile([P, BLOCKS, 2 * BATCH], F32)
         slope = keep.tile([P, BLOCKS, BATCH], F32)
@@ -81,57 +86,74 @@ def tile_causalfeaturetransformer_pa_kernel(
         result = [keep.tile([P, D_OUT], F32, name="result%d" % b) for b in range(2 * UNITS)]
         unbiased = {c: keep.tile([P, D_OUT], F32, name="unbiased%d" % c) for c in range(HELP_FROM, PAIRS)}
 
-        def by_slot(x):
-            return x.rearrange("q (p t) -> q t p", t=PACK)
+        def by_word(x):
+            return x.rearrange("q (p u e) -> q u p e", u=2, e=2)
 
         def as_they_lie(x):
-            return x.rearrange("q (t p) -> q t p", t=PACK)
+            return x.rearrange("q (u p e) -> q u p e", u=2, e=2)
 
-        def spread_row(rows, r, view):
+        def spread_row(rows, r):
             bank = acc_banks.tile([P, D_EMB], F32, name="acc")
             nc.tensor.matmul(
-                out=bank[:].rearrange("q (t p) -> q t p", t=PACK),
+                out=as_they_lie(bank[:]),
                 lhsT=ident_bf[:, r : r + 1].to_broadcast([P, P]),
-                rhs=view(rows[:]),
+                rhs=by_word(rows[:]),
                 start=True,
                 stop=True,
             )
             return bank
 
-        def turn_z_terms(first, end):
-            bank = turned_banks.tile([P, BLOCKS, P], F32, name="turned")
-            nc.tensor.transpose(bank[:, 0, :], z_terms[:, 0:P], ident[:])
-            for j in range(first, end):
-                nc.tensor.transpose(bank[:, 1 + j - first, :], z_terms[:, (1 + j) * P : (2 + j) * P], ident[:])
-            return bank
+        def turn_f(bank):
+            for j in range(BLOCKS):
+                nc.tensor.transpose(
+                    bank[:, BATCH * j : BATCH * j + P], f_rows[:, j * P : (j + 1) * P], ident[:]
+                )
+            return bank[:, 0 : BLOCKS * BATCH].rearrange("p (j n) -> p j n", n=BATCH)
 
-        def measure(j):
-            nc.vector.bn_stats(out=e_stats[:, j, :], in_=emb[:, j, :])
-            nc.vector.bn_aggr(out=e_mv[:, j, :], in_=e_stats[:, j, :])
+        def measure_on_vector(j):
+            nc.vector.bn_stats(out=e_stats[:], in_=emb[:, j, :])
+            nc.vector.bn_aggr(out=e_mv[:, j, :], in_=e_stats[:])
 
-        def shape(j):
-            nc.vector.scalar_tensor_tensor(
-                out=shaped[:, j, :].rearrange("q (t p) -> q t p", t=PACK),
-                in0=by_slot(emb[:, j, :]),
-                scalar=e_mv[:, j, 0:1],
-                in1=g1_bank[:].rearrange("q (t p) -> q t p", t=PACK),
-                op0=ALU.subtract,
-                op1=ALU.mult,
+        def measure_on_scalar(j):
+            nc.scalar.activation(
+                out=unused[:], in_=emb[:, j, :], func=ACT.Copy, scale=1.0 / D_EMB, accum_out=e_mv[:, j, 0:1]
+            )
+            nc.scalar.activation(
+                out=unused[:],
+                in_=emb[:, j, :],
+                func=ACT.Square,
+                scale=-1.0,
+                bias=e_mv[:, j, 0:1],
+                accum_out=e_squares[:, j : j + 1],
+            )
+            nc.scalar.activation(
+                out=e_mv[:, j, 1:2], in_=e_squares[:, j : j + 1], func=ACT.Copy, scale=1.0 / D_EMB
             )
 
-        def slope_root(first, end, bank):
-            some = [P, end - first, BATCH]
-            d = bank[:, 1 : 1 + end - first, 0:BATCH]
-            part = root[:, first:end, 0:BATCH]
-            nc.vector.tensor_mul(out=part, in0=d, in1=e_mv[:, first:end, 1:2].to_broadcast(some))
-            nc.vector.tensor_mul(out=part, in0=d, in1=part)
-            nc.vector.tensor_add(out=part, in0=bank[:, 0:1, 0:BATCH].to_broadcast(some), in1=part)
-            nc.scalar.activation(out=part, in_=part, func=ACT.Sqrt)
+        def shape(j):
+            for u in range(2):
+                nc.vector.scalar_tensor_tensor(
+                    out=as_they_lie(shaped[:, j, :])[:, u],
+                    in0=by_word(emb[:, j, :])[:, u],
+                    scalar=e_mv[:, j, 0:1],
+                    in1=as_they_lie(g1_bank[:])[:, u],
+                    op0=ALU.subtract,
+                    op1=ALU.mult,
+                )
 
-        def slope_divide(first, end, bank):
-            part = root[:, first:end, 0:BATCH]
-            nc.vector.reciprocal(out=part, in_=part)
-            nc.vector.tensor_mul(out=slope[:, first:end, :], in0=bank[:, 1 : 1 + end - first, 0:BATCH], in1=part)
+        def find_root(j):
+            nc.scalar.activation(
+                out=root[:, j, 0:BATCH],
+                in_=f_squared[:, j, :],
+                func=ACT.Abs_reciprocal_sqrt,
+                scale=e_mv[:, j, 1:2],
+                bias=EPS,
+            )
+
+        def find_slopes(first, end):
+            nc.vector.tensor_mul(
+                out=slope[:, first:end, :], in0=f[:, first:end, :], in1=root[:, first:end, 0:BATCH]
+            )
 
         def regroup_weight(w):
             nc.gpsimd.tensor_scalar(
@@ -166,16 +188,22 @@ def tile_causalfeaturetransformer_pa_kernel(
             nc.scalar.activation(
                 out=scaled[u][:], in_=shaped[:, j, :], func=ACT.Copy, scale=slope[:, j, n : n + 1]
             )
-            nc.gpsimd.tensor_tensor(out=xn[u][:], in0=scaled[u][:], in1=be1_all[:], op=ALU.add)
+            nc.gpsimd.tensor_tensor(
+                out=as_they_lie(xn[u][:]), in0=as_they_lie(scaled[u][:]), in1=by_word(be1_all[:]), op=ALU.add
+            )
 
         def turn_and_regroup(c):
-            turned = turned_banks.tile([P, PAIR, PACK, P], BF16)
+            turned = turned_banks.tile([P, PAIR, 2, P], F32, name="turned")
             for h in range(PAIR):
-                for t in range(PACK):
-                    nc.tensor.transpose(
-                        turned[:, h, t, :], xn[PAIR * c + h][:, t * P : (t + 1) * P], ident_bf[:]
-                    )
-            nc.scalar.copy(out=x_grouped[c][:], in_=turned[:].rearrange("p h t r -> p h r t"))
+                words = xn[PAIR * c + h][:].bitcast(F32)
+                for u in range(2):
+                    nc.tensor.transpose(turned[:, h, u, :], words[:, u * P : (u + 1) * P], ident[:])
+            nc.scalar.copy(
+                out=x_grouped[c][:].rearrange("p h r t -> p (h r t)").bitcast(F32).rearrange(
+                    "p (h r u) -> p h r u", h=PAIR, u=2
+                ),
+                in_=turned[:].rearrange("p h u r -> p h r u"),
+            )
 
         def quantise(c):
             nc.vector.quantize_mx(
@@ -186,9 +214,9 @@ def tile_causalfeaturetransformer_pa_kernel(
 
         def multiply(c):
             banks = []
-            for h in range(PAIR):
-                tokens = slice(h * P, (h + 1) * P)
-                for w in range(2):
+            for w in range(2):
+                for h in range(PAIR):
+                    tokens = slice(h * P, (h + 1) * P)
                     acc = acc_banks.tile([P, D_OUT], F32)
                     nc.tensor.matmul_mx(
                         out=acc[:],
@@ -203,115 +231,120 @@ def tile_causalfeaturetransformer_pa_kernel(
             return banks
 
         def add_bias_on_vector(c, b, banks):
-            nc.vector.tensor_add(out=result[PAIR_BANKS * c + b][:], in0=banks[b][:], in1=bias_all[b % 2][:])
+            nc.vector.tensor_add(out=result[PAIR_BANKS * c + b][:], in0=banks[b][:], in1=bias_all[b // 2][:])
 
         def add_bias_on_scalar_and_gpsimd(c, b, banks):
             nc.scalar.copy(out=unbiased[c][:], in_=banks[b][:])
             nc.gpsimd.tensor_tensor(
-                out=result[PAIR_BANKS * c + b][:], in0=unbiased[c][:], in1=bias_all[b % 2][:], op=ALU.add
+                out=result[PAIR_BANKS * c + b][:], in0=unbiased[c][:], in1=bias_all[b // 2][:], op=ALU.add
             )
 
         def store(c, b):
-            j, n = divmod(PAIR * c + b // 2, BATCH)
-            nc.sync.dma_start(out=outs[b % 2][n, j * P : (j + 1) * P, :], in_=result[PAIR_BANKS * c + b][:])
+            j, n = divmod(PAIR * c + b % 2, BATCH)
+            nc.sync.dma_start(out=outs[b // 2][n, j * P : (j + 1) * P, :], in_=result[PAIR_BANKS * c + b][:])
 
         def load_row(rows, r, vector):
             nc.sync.dma_start(out=rows[r : r + 1, :], in_=vector.rearrange("(a k) -> a k", a=1))
 
+        def load_block(j):
+            nc.sync.dma_start(out=emb[:, j, :], in_=feat_emb[j * P : (j + 1) * P, :])
+
         def load_weight(w):
             nc.sync.dma_start(out=w_raw[w][:], in_=weights[w].rearrange("(p t) n -> p t n", p=P))
 
-        nc.vector.memset(norm_rows[:], 0.0)
-        nc.vector.memset(bias_rows[:], 0.0)
+        nc.gpsimd.memset(norm_rows[:].bitcast(I32), 0)
+        nc.gpsimd.memset(warm[:], 1.0)
         nc.sync.dma_start(out=z_rows[0:BATCH, 0:D_FEAT], in_=Z)
-        nc.sync.dma_start(out=emb[:, 0, :], in_=feat_emb[0:P, :])
+        load_block(0)
         load_row(norm_rows, 0, g1)
         load_row(norm_rows, 1, be1)
-        nc.sync.dma_start(out=emb[:, 1, :], in_=feat_emb[P : 2 * P, :])
-        nc.sync.dma_start(out=emb[:, 2, :], in_=feat_emb[2 * P : 3 * P, :])
+        load_block(1)
         load_weight(0)
+        load_block(2)
         load_weight(1)
-        load_row(bias_rows, 0, bk)
-        load_row(bias_rows, 1, bv)
         last = (BLOCKS - 1) * P
         nc.sync.dma_start(out=emb[0:112, BLOCKS - 1, :], in_=feat_emb[last : last + 112, :])
         nc.sync.dma_start(out=emb[112:127, BLOCKS - 1, :], in_=feat_emb[last + 112 : D_FEAT, :])
         nc.sync.dma_start(
             out=emb[127:128, BLOCKS - 1, :], in_=label_token.rearrange("a b k -> (a b) k")
         )
+        nc.sync.dma_start(out=be1_all[:], in_=be1.partition_broadcast(P))
+        for w in range(2):
+            nc.sync.dma_start(out=bias_all[w][:], in_=biases[w].partition_broadcast(P))
 
+        make_identity(nc, ident_bf[:])
+        nc.gpsimd.memset(f_rows[:], 0.0)
         make_identity(nc, ident[:])
-        nc.gpsimd.memset(z_terms[:], 0.0)
-        nc.vector.memset(warm[:], 1.0)
-        nc.scalar.activation(out=warm[:], in_=warm[:], func=ACT.Sqrt)
-        nc.vector.tensor_copy(out=ident_bf[:], in_=ident[:])
+        nc.scalar.activation(out=warm[:], in_=warm[:], func=ACT.Abs_reciprocal_sqrt)
 
         rows4 = slice(0, BATCH)
+        nc.vector.memset(f_rows[rows4, D_FEAT:SEQ], 1.0)
         nc.vector.bn_stats(out=z_stats[rows4, :], in_=z_rows[rows4, 0:D_FEAT])
         nc.vector.bn_aggr(out=z_mv[rows4, :], in_=z_stats[rows4, :])
-        nc.vector.tensor_scalar_sub(
-            out=z_terms[rows4, P : P + D_FEAT], in0=z_rows[rows4, 0:D_FEAT], scalar1=z_mv[rows4, 0:1]
+        nc.scalar.activation(
+            out=z_rstd[rows4, :], in_=z_mv[rows4, 1:2], func=ACT.Abs_reciprocal_sqrt, bias=EPS
         )
+        measure_on_vector(0)
         nc.vector.tensor_scalar(
-            out=z_terms[rows4, 0:P],
-            in0=z_mv[rows4, 1:2].to_broadcast([BATCH, P]),
-            scalar1=EPS,
-            scalar2=EPS,
-            op0=ALU.add,
+            out=f_rows[rows4, 0:D_FEAT],
+            in0=z_rows[rows4, 0:D_FEAT],
+            scalar1=z_mv[rows4, 0:1],
+            scalar2=z_rstd[rows4, 0:1],
+            op0=ALU.subtract,
             op1=ALU.mult,
         )
-        nc.vector.tensor_scalar_add(out=z_var_eps[rows4, :], in0=z_mv[rows4, 1:2], scalar1=EPS)
-        g1_bank = spread_row(norm_rows, 0, by_slot)
-        be1_bank = spread_row(norm_rows, 1, by_slot)
-        nc.scalar.copy(out=be1_all[:], in_=be1_bank[:])
-        nc.scalar.activation(
-            out=z_terms[rows4, P + D_FEAT : P + SEQ], in_=z_var_eps[rows4, :], func=ACT.Sqrt
-        )
+        g1_bank = spread_row(norm_rows, 0)
+        be1_bank = spread_row(norm_rows, 1)
         regroup_weight(0)
         regroup_weight(1)
-        early = BLOCKS // 2
-        early_bank = turn_z_terms(0, early)
-        late_bank = turn_z_terms(early, BLOCKS)
-        for j in range(early):
-            measure(j)
-        slope_root(0, early, early_bank)
+        measure_on_scalar(1)
+        f_bank = turned_banks.tile([P, D_EMB], F32, name="turned")
+        turned_f = turn_f(f_bank)
         shape(0)
+        nc.scalar.activation(out=f_squared[:], in_=turned_f, func=ACT.Square)
+        nc.vector.tensor_copy(out=f[:], in_=turned_f)
+        find_root(0)
+        find_root(1)
         shape(1)
-        slope_divide(0, early, early_bank)
-        for u in range(VECTOR_UNITS, 2 * VECTOR_UNITS):
-            form_on_scalar_and_gpsimd(u)
+        find_slopes(0, 2)
+        measure_on_scalar(2)
         form_on_vector(0)
         form_on_vector(1)
-        for j in range(early, BLOCKS):
-            measure(j)
-        slope_root(early, BLOCKS, late_bank)
-        turn_and_regroup(0)
-        for w in range(2):
-            nc.scalar.copy(out=bias_all[w][:], in_=spread_row(bias_rows, w, as_they_lie)[:])
+        form_on_scalar_and_gpsimd(4)
+        form_on_scalar_and_gpsimd(5)
         form_on_vector(2)
-        form_on_vector(3)
-        shape(2)
-        slope_divide(early, BLOCKS, late_bank)
-        turn_and_regroup(1)
+        turn_and_regroup(0)
         quantise_weight(0)
-        quantise_weight(1)
+        form_on_vector(3)
+        form_on_scalar_and_gpsimd(6)
         quantise(0)
-        shape(3)
+        measure_on_scalar(3)
+        find_root(2)
+        find_root(3)
+        turn_and_regroup(1)
+        form_on_scalar_and_gpsimd(7)
+        quantise_weight(1)
 
         for step in range(PAIRS):
             banks = multiply(step)
-            if step + FORM_AHEAD < PAIRS:
-                for h in range(PAIR):
-                    form_on_scalar_and_gpsimd(PAIR * (step + FORM_AHEAD) + h)
             helped = step >= HELP_FROM
             if helped:
                 add_bias_on_scalar_and_gpsimd(step, 0, banks)
-            if step + TURN_AHEAD < PAIRS:
-                turn_and_regroup(step + TURN_AHEAD)
             for b in range(1 if helped else 0, PAIR_BANKS):
                 if b == 1 and step + 1 < PAIRS:
                     quantise(step + 1)
                 add_bias_on_vector(step, b, banks)
                 store(step, b)
-                if helped and b == PAIR_BANKS // 2:
-                    store(step, 0)
+                if step == 0 and b == 1:
+                    shape(2)
+                    find_slopes(2, BLOCKS)
+                if step == 0 and b == 2:
+                    shape(3)
+            if step - 1 >= HELP_FROM:
+                store(step - 1, 0)
+            if step + FORM_AHEAD < PAIRS:
+                for h in range(PAIR):
+                    form_on_scalar_and_gpsimd(PAIR * (step + FORM_AHEAD) + h)
+            if step + TURN_AHEAD < PAIRS:
+                turn_and_regroup(step + TURN_AHEAD)
+        store(PAIRS - 1, 0)

@@ -188,9 +188,7 @@ def tile_causalfeaturetransformer_pa_kernel(
             nc.scalar.activation(
                 out=scaled[u][:], in_=shaped[:, j, :], func=ACT.Copy, scale=slope[:, j, n : n + 1]
             )
-            nc.gpsimd.tensor_tensor(
-                out=as_they_lie(xn[u][:]), in0=as_they_lie(scaled[u][:]), in1=by_word(be1_all[:]), op=ALU.add
-            )
+            nc.gpsimd.tensor_tensor(out=xn[u][:], in0=scaled[u][:], in1=be1_all[:], op=ALU.add)
 
         def turn_and_regroup(c):
             turned = turned_banks.tile([P, PAIR, 2, P], F32, name="turned")
@@ -268,7 +266,6 @@ def tile_causalfeaturetransformer_pa_kernel(
         nc.sync.dma_start(
             out=emb[127:128, BLOCKS - 1, :], in_=label_token.rearrange("a b k -> (a b) k")
         )
-        nc.sync.dma_start(out=be1_all[:], in_=be1.partition_broadcast(P))
         for w in range(2):
             nc.sync.dma_start(out=bias_all[w][:], in_=biases[w].partition_broadcast(P))
 
@@ -305,6 +302,7 @@ def tile_causalfeaturetransformer_pa_kernel(
         nc.vector.tensor_copy(out=f[:], in_=turned_f)
         find_root(0)
         find_root(1)
+        nc.scalar.copy(out=be1_all[:], in_=be1_bank[:])
         shape(1)
         find_slopes(0, 2)
         measure_on_scalar(2)

@@ -19,17 +19,15 @@ D_FEAT = 511
 SEQ = D_FEAT + 1
 D_EMB = 512
 D_OUT = 512
-BLOCKS = SEQ // P
 EPS = 1e-5
+HALF = SEQ // 2
+SIDES = 2
+BLOCKS = 2 * SIDES
+PAIRS = 2 * BATCH
 
-UNITS = BLOCKS * BATCH
-PAIR = 2
-PAIRS = UNITS // PAIR
-PAIR_BANKS = 2 * PAIR
-VECTOR_UNITS = BATCH
 TURN_AHEAD = 2
-FORM_AHEAD = 4
-HELP_FROM = PAIRS - FORM_AHEAD - 1
+FORM_AHEAD = 3
+VECTOR_PAIRS = 1
 
 FLOPS = 2 * BATCH * SEQ * D_EMB * 2 * D_OUT
 
@@ -39,7 +37,6 @@ def tile_causalfeaturetransformer_pa_kernel(
 ):
     nc = tc.nc
     weights = (wk, wv)
-    biases = (bk, bv)
     outs = (out_0, out_1)
 
     with ExitStack() as ctx:
@@ -52,13 +49,12 @@ def tile_causalfeaturetransformer_pa_kernel(
         ident_bf = keep.tile([P, P], BF16)
         warm = keep.tile([P, 1], F32)
         z_rows = keep.tile([P, SEQ], BF16)
-        norm_rows = keep.tile([P, D_EMB], BF16)
+        rows = keep.tile([P, D_EMB], BF16)
         emb = keep.tile([P, BLOCKS, D_EMB], BF16)
         z_stats = keep.tile([P, 6], F32)
         z_mv = keep.tile([P, 2], F32)
         z_rstd = keep.tile([P, 1], F32)
         f_rows = keep.tile([P, SEQ], F32)
-        f = keep.tile([P, BLOCKS, BATCH], F32)
         f_squared = keep.tile([P, BLOCKS, BATCH], F32)
         e_stats = keep.tile([P, 6], F32)
         e_mv = keep.tile([P, BLOCKS, 2], F32)
@@ -67,7 +63,7 @@ def tile_causalfeaturetransformer_pa_kernel(
         shaped = keep.tile([P, BLOCKS, D_EMB], F32)
         root = keep.tile([P, BLOCKS, 2 * BATCH], F32)
         slope = keep.tile([P, BLOCKS, BATCH], F32)
-        be1_all = keep.tile([P, D_EMB], BF16)
+        be1_all = keep.tile([P, PACK, P], F32)
         bias_all = [keep.tile([P, D_OUT], BF16, name="bias_all%d" % w) for w in range(2)]
         w_raw = [keep.tile([P, PACK, D_OUT], BF16, name="w_raw%d" % w) for w in range(2)]
         w_grouped = [
@@ -75,16 +71,22 @@ def tile_causalfeaturetransformer_pa_kernel(
         ]
         w_codes = [keep.tile([P, D_OUT], U32, name="w_codes%d" % w, align_bytes=64) for w in range(2)]
         w_scales = [keep.tile([P, D_OUT], U8, name="w_scales%d" % w, align_bytes=64) for w in range(2)]
-        scaled = {u: keep.tile([P, D_EMB], F32, name="scaled%d" % u) for u in range(VECTOR_UNITS, UNITS)}
-        xn = [keep.tile([P, D_EMB], BF16, name="xn%d" % u) for u in range(UNITS)]
+        xn = {
+            (c, h): keep.tile([P, D_EMB], BF16, name="xn%d_%d" % (c, h))
+            for c in range(VECTOR_PAIRS) for h in range(SIDES)
+        }
+        scaled = {
+            (c, h): keep.tile([P, PACK, P], F32, name="scaled%d_%d" % (c, h))
+            for c in range(VECTOR_PAIRS, PAIRS) for h in range(SIDES)
+        }
         x_grouped = [
-            keep.tile([P, PAIR, P, PACK], BF16, name="x_grouped%d" % c, align_bytes=64)
-            for c in range(PAIRS)
+            keep.tile([P, SIDES, P, PACK], BF16, name="x_grouped%d" % c, align_bytes=64) for c in range(PAIRS)
         ]
-        x_codes = [keep.tile([P, PAIR * P], U32, name="x_codes%d" % c, align_bytes=64) for c in range(PAIRS)]
-        x_scales = [keep.tile([P, PAIR * P], U8, name="x_scales%d" % c, align_bytes=64) for c in range(PAIRS)]
-        result = [keep.tile([P, D_OUT], F32, name="result%d" % b) for b in range(2 * UNITS)]
-        unbiased = {c: keep.tile([P, D_OUT], F32, name="unbiased%d" % c) for c in range(HELP_FROM, PAIRS)}
+        x_codes = [keep.tile([P, SIDES * P], U32, name="x_codes%d" % c, align_bytes=64) for c in range(PAIRS)]
+        x_scales = [keep.tile([P, SIDES * P], U8, name="x_scales%d" % c, align_bytes=64) for c in range(PAIRS)]
+        result = [
+            [keep.tile([P, SIDES, D_OUT], F32, name="result%d_%d" % (c, w)) for w in range(2)] for c in range(PAIRS)
+        ]
 
         def by_word(x):
             return x.rearrange("q (p u e) -> q u p e", u=2, e=2)
@@ -92,7 +94,7 @@ def tile_causalfeaturetransformer_pa_kernel(
         def as_they_lie(x):
             return x.rearrange("q (u p e) -> q u p e", u=2, e=2)
 
-        def spread_row(rows, r):
+        def spread_row(r):
             bank = acc_banks.tile([P, D_EMB], F32, name="acc")
             nc.tensor.matmul(
                 out=as_they_lie(bank[:]),
@@ -103,10 +105,12 @@ def tile_causalfeaturetransformer_pa_kernel(
             )
             return bank
 
-        def turn_f(bank):
+        def turn_f():
+            bank = acc_banks.tile([P, D_EMB], F32, name="acc")
             for j in range(BLOCKS):
+                half, h = divmod(j, SIDES)
                 nc.tensor.transpose(
-                    bank[:, BATCH * j : BATCH * j + P], f_rows[:, j * P : (j + 1) * P], ident[:]
+                    bank[:, BATCH * j : BATCH * j + P], f_rows[:, half * HALF + h : (half + 1) * HALF : SIDES], ident[:]
                 )
             return bank[:, 0 : BLOCKS * BATCH].rearrange("p (j n) -> p j n", n=BATCH)
 
@@ -119,40 +123,33 @@ def tile_causalfeaturetransformer_pa_kernel(
                 out=unused[:], in_=emb[:, j, :], func=ACT.Copy, scale=1.0 / D_EMB, accum_out=e_mv[:, j, 0:1]
             )
             nc.scalar.activation(
-                out=unused[:],
-                in_=emb[:, j, :],
-                func=ACT.Square,
-                scale=-1.0,
-                bias=e_mv[:, j, 0:1],
+                out=unused[:], in_=emb[:, j, :], func=ACT.Square, scale=-1.0, bias=e_mv[:, j, 0:1],
                 accum_out=e_squares[:, j : j + 1],
             )
             nc.scalar.activation(
                 out=e_mv[:, j, 1:2], in_=e_squares[:, j : j + 1], func=ACT.Copy, scale=1.0 / D_EMB
             )
 
-        def shape(j):
+        def shape(j, gain):
             for u in range(2):
                 nc.vector.scalar_tensor_tensor(
                     out=as_they_lie(shaped[:, j, :])[:, u],
                     in0=by_word(emb[:, j, :])[:, u],
                     scalar=e_mv[:, j, 0:1],
-                    in1=as_they_lie(g1_bank[:])[:, u],
+                    in1=as_they_lie(gain[:])[:, u],
                     op0=ALU.subtract,
                     op1=ALU.mult,
                 )
 
         def find_root(j):
             nc.scalar.activation(
-                out=root[:, j, 0:BATCH],
-                in_=f_squared[:, j, :],
-                func=ACT.Abs_reciprocal_sqrt,
-                scale=e_mv[:, j, 1:2],
-                bias=EPS,
+                out=root[:, j, 0:BATCH], in_=f_squared[:, j, :], func=ACT.Abs_reciprocal_sqrt,
+                scale=e_mv[:, j, 1:2], bias=EPS,
             )
 
-        def find_slopes(first, end):
+        def find_slopes(first, end, f_of):
             nc.vector.tensor_mul(
-                out=slope[:, first:end, :], in0=f[:, first:end, :], in1=root[:, first:end, 0:BATCH]
+                out=slope[:, first:end, :], in0=f_of[:, first:end, :], in1=root[:, first:end, 0:BATCH]
             )
 
         def regroup_weight(w):
@@ -172,36 +169,52 @@ def tile_causalfeaturetransformer_pa_kernel(
                 in_=w_grouped[w][:].rearrange("p n t -> p (n t)"),
             )
 
-        def form_on_vector(u):
-            j, n = divmod(u, BATCH)
-            nc.vector.scalar_tensor_tensor(
-                out=xn[u][:],
-                in0=shaped[:, j, :],
-                scalar=slope[:, j, n : n + 1],
-                in1=be1_bank[:],
-                op0=ALU.mult,
-                op1=ALU.add,
-            )
+        def form(c):
+            half, n = divmod(c, BATCH)
+            for h in range(SIDES):
+                j = SIDES * half + h
+                if c < VECTOR_PAIRS:
+                    nc.vector.scalar_tensor_tensor(
+                        out=xn[c, h][:], in0=shaped[:, j, :], scalar=slope[:, j, n : n + 1], in1=be1_bank[:],
+                        op0=ALU.mult, op1=ALU.add,
+                    )
+                    continue
+                out = scaled[c, h][:].rearrange("q (u e) p -> q u e p", u=2)
+                in_ = shaped[:, j, :].rearrange("q (u p e) -> q u e p", u=2, e=2)
+                nc.scalar.activation(out=out, in_=in_, func=ACT.Copy, scale=slope[:, j, n : n + 1])
 
-        def form_on_scalar_and_gpsimd(u):
-            j, n = divmod(u, BATCH)
-            nc.scalar.activation(
-                out=scaled[u][:], in_=shaped[:, j, :], func=ACT.Copy, scale=slope[:, j, n : n + 1]
-            )
-            nc.gpsimd.tensor_tensor(out=xn[u][:], in0=scaled[u][:], in1=be1_all[:], op=ALU.add)
-
-        def turn_and_regroup(c):
-            turned = turned_banks.tile([P, PAIR, 2, P], F32, name="turned")
-            for h in range(PAIR):
-                words = xn[PAIR * c + h][:].bitcast(F32)
+        def turn_words(c):
+            turned = turned_banks.tile([P, SIDES, 2, P], F32, name="turned")
+            for h in range(SIDES):
+                words = xn[c, h][:].bitcast(F32)
                 for u in range(2):
                     nc.tensor.transpose(turned[:, h, u, :], words[:, u * P : (u + 1) * P], ident[:])
             nc.scalar.copy(
                 out=x_grouped[c][:].rearrange("p h r t -> p (h r t)").bitcast(F32).rearrange(
-                    "p (h r u) -> p h r u", h=PAIR, u=2
+                    "p (h r u) -> p h r u", h=SIDES, u=2
                 ),
                 in_=turned[:].rearrange("p h u r -> p h r u"),
             )
+
+        def turn_and_add(c, h):
+            turned = turned_banks.tile([P, PACK, P], F32, name="turned")
+            for t in range(PACK):
+                nc.tensor.matmul(
+                    out=turned[:, t, :], lhsT=be1_all[:, t, :], rhs=ident[:], start=True, stop=False,
+                    is_transpose=True,
+                )
+                nc.tensor.matmul(
+                    out=turned[:, t, :], lhsT=scaled[c, h][:, t, :], rhs=ident[:], start=False, stop=True,
+                    is_transpose=True,
+                )
+            nc.scalar.copy(out=x_grouped[c][:, h], in_=turned[:].rearrange("p t r -> p r t"))
+
+        def turn(c):
+            if c < VECTOR_PAIRS:
+                turn_words(c)
+            else:
+                for h in range(SIDES):
+                    turn_and_add(c, h)
 
         def quantise(c):
             nc.vector.quantize_mx(
@@ -210,64 +223,53 @@ def tile_causalfeaturetransformer_pa_kernel(
                 in_=x_grouped[c][:].rearrange("p h r t -> p (h r t)"),
             )
 
-        def multiply(c):
+        def multiply(c, w):
             banks = []
-            for w in range(2):
-                for h in range(PAIR):
-                    tokens = slice(h * P, (h + 1) * P)
-                    acc = acc_banks.tile([P, D_OUT], F32)
-                    nc.tensor.matmul_mx(
-                        out=acc[:],
-                        lhsT=x_codes[c][:, tokens].bitcast(FP8X4),
-                        lhsT_scale=x_scales[c][:, tokens],
-                        rhs=w_codes[w][:].bitcast(FP8X4),
-                        rhs_scale=w_scales[w][:],
-                        start=True,
-                        stop=True,
-                    )
-                    banks.append(acc)
+            for h in range(SIDES):
+                tokens = slice(h * P, (h + 1) * P)
+                acc = acc_banks.tile([P, D_OUT], F32, name="acc")
+                nc.tensor.matmul_mx(
+                    out=acc[:],
+                    lhsT=x_codes[c][:, tokens].bitcast(FP8X4),
+                    lhsT_scale=x_scales[c][:, tokens],
+                    rhs=w_codes[w][:].bitcast(FP8X4),
+                    rhs_scale=w_scales[w][:],
+                    start=True,
+                    stop=True,
+                )
+                banks.append(acc)
             return banks
 
-        def add_bias_on_vector(c, b, banks):
-            nc.vector.tensor_add(out=result[PAIR_BANKS * c + b][:], in0=banks[b][:], in1=bias_all[b // 2][:])
+        def add_bias(c, w, h, banks):
+            nc.vector.tensor_add(out=result[c][w][:, h, :], in0=banks[h][:], in1=bias_all[w][:])
 
-        def add_bias_on_scalar_and_gpsimd(c, b, banks):
-            nc.scalar.copy(out=unbiased[c][:], in_=banks[b][:])
-            nc.gpsimd.tensor_tensor(
-                out=result[PAIR_BANKS * c + b][:], in0=unbiased[c][:], in1=bias_all[b // 2][:], op=ALU.add
-            )
+        def store(c, w, sides=slice(0, SIDES)):
+            half, n = divmod(c, BATCH)
+            out = outs[w][n, half * HALF : (half + 1) * HALF, :].rearrange("(p h) k -> p h k", h=SIDES)
+            nc.sync.dma_start(out=out[:, sides, :], in_=result[c][w][:, sides, :])
 
-        def store(c, b):
-            j, n = divmod(PAIR * c + b % 2, BATCH)
-            nc.sync.dma_start(out=outs[b // 2][n, j * P : (j + 1) * P, :], in_=result[PAIR_BANKS * c + b][:])
-
-        def load_row(rows, r, vector):
+        def load_row(r, vector):
             nc.sync.dma_start(out=rows[r : r + 1, :], in_=vector.rearrange("(a k) -> a k", a=1))
-
-        def load_block(j):
-            nc.sync.dma_start(out=emb[:, j, :], in_=feat_emb[j * P : (j + 1) * P, :])
 
         def load_weight(w):
             nc.sync.dma_start(out=w_raw[w][:], in_=weights[w].rearrange("(p t) n -> p t n", p=P))
 
-        nc.gpsimd.memset(norm_rows[:].bitcast(I32), 0)
+        nc.gpsimd.memset(rows[:].bitcast(I32), 0)
         nc.gpsimd.memset(warm[:], 1.0)
         nc.sync.dma_start(out=z_rows[0:BATCH, 0:D_FEAT], in_=Z)
-        load_block(0)
-        load_row(norm_rows, 0, g1)
-        load_row(norm_rows, 1, be1)
-        load_block(1)
-        load_weight(0)
-        load_block(2)
-        load_weight(1)
-        last = (BLOCKS - 1) * P
-        nc.sync.dma_start(out=emb[0:112, BLOCKS - 1, :], in_=feat_emb[last : last + 112, :])
-        nc.sync.dma_start(out=emb[112:127, BLOCKS - 1, :], in_=feat_emb[last + 112 : D_FEAT, :])
         nc.sync.dma_start(
-            out=emb[127:128, BLOCKS - 1, :], in_=label_token.rearrange("a b k -> (a b) k")
+            out=emb[:, 0:SIDES, :], in_=feat_emb[0:HALF, :].rearrange("(p h) k -> p h k", h=SIDES)
         )
-        for w in range(2):
-            nc.sync.dma_start(out=bias_all[w][:], in_=biases[w].partition_broadcast(P))
+        load_row(0, g1)
+        load_row(1, be1)
+        load_weight(0)
+        nc.sync.dma_start(out=emb[:, SIDES, :], in_=feat_emb[HALF:D_FEAT:SIDES, :])
+        load_weight(1)
+        nc.sync.dma_start(out=emb[0:112, SIDES + 1, :], in_=feat_emb[HALF + 1 : HALF + 1 + 2 * 112 : SIDES, :])
+        nc.sync.dma_start(out=emb[112:127, SIDES + 1, :], in_=feat_emb[HALF + 1 + 2 * 112 : D_FEAT : SIDES, :])
+        nc.sync.dma_start(out=emb[127:128, SIDES + 1, :], in_=label_token.rearrange("a b k -> (a b) k"))
+        nc.sync.dma_start(out=bias_all[0][:], in_=bk.partition_broadcast(P))
+        nc.sync.dma_start(out=bias_all[1][:], in_=bv.partition_broadcast(P))
 
         make_identity(nc, ident_bf[:])
         nc.gpsimd.memset(f_rows[:], 0.0)
@@ -281,68 +283,57 @@ def tile_causalfeaturetransformer_pa_kernel(
         nc.scalar.activation(
             out=z_rstd[rows4, :], in_=z_mv[rows4, 1:2], func=ACT.Abs_reciprocal_sqrt, bias=EPS
         )
-        measure_on_vector(0)
+        nc.vector.bn_stats(out=e_stats[:], in_=emb[:, 0, :])
         nc.vector.tensor_scalar(
-            out=f_rows[rows4, 0:D_FEAT],
-            in0=z_rows[rows4, 0:D_FEAT],
-            scalar1=z_mv[rows4, 0:1],
-            scalar2=z_rstd[rows4, 0:1],
-            op0=ALU.subtract,
-            op1=ALU.mult,
+            out=f_rows[rows4, 0:D_FEAT], in0=z_rows[rows4, 0:D_FEAT], scalar1=z_mv[rows4, 0:1],
+            scalar2=z_rstd[rows4, 0:1], op0=ALU.subtract, op1=ALU.mult,
         )
-        g1_bank = spread_row(norm_rows, 0)
-        be1_bank = spread_row(norm_rows, 1)
+        nc.vector.bn_aggr(out=e_mv[:, 0, :], in_=e_stats[:])
+        be1_bank = spread_row(1)
+        g1_bank = spread_row(0)
+        measure_on_scalar(1)
+        turned_f = turn_f()
         regroup_weight(0)
         regroup_weight(1)
-        measure_on_scalar(1)
-        f_bank = turned_banks.tile([P, D_EMB], F32, name="turned")
-        turned_f = turn_f(f_bank)
-        shape(0)
+        shape(0, g1_bank)
         nc.scalar.activation(out=f_squared[:], in_=turned_f, func=ACT.Square)
-        nc.vector.tensor_copy(out=f[:], in_=turned_f)
         find_root(0)
         find_root(1)
-        nc.scalar.copy(out=be1_all[:], in_=be1_bank[:])
-        shape(1)
-        find_slopes(0, 2)
-        measure_on_scalar(2)
-        form_on_vector(0)
-        form_on_vector(1)
-        form_on_scalar_and_gpsimd(4)
-        form_on_scalar_and_gpsimd(5)
-        form_on_vector(2)
-        turn_and_regroup(0)
-        quantise_weight(0)
-        form_on_vector(3)
-        form_on_scalar_and_gpsimd(6)
-        quantise(0)
-        measure_on_scalar(3)
+        nc.scalar.copy(
+            out=be1_all[:].rearrange("q (u e) p -> q u e p", u=2),
+            in_=be1_bank[:].rearrange("q (u p e) -> q u e p", u=2, e=2),
+        )
+        shape(1, g1_bank)
+        measure_on_vector(2)
+        find_slopes(0, 2, turned_f)
+        form(0)
+        form(1)
+        turn(0)
         find_root(2)
+        measure_on_vector(3)
+        shape(2, g1_bank)
+        shape(3, g1_bank)
         find_root(3)
-        turn_and_regroup(1)
-        form_on_scalar_and_gpsimd(7)
+        turn(1)
+        quantise_weight(0)
+        quantise(0)
         quantise_weight(1)
-
+        find_slopes(2, 4, turned_f)
+        form(2)
         for step in range(PAIRS):
-            banks = multiply(step)
-            helped = step >= HELP_FROM
-            if helped:
-                add_bias_on_scalar_and_gpsimd(step, 0, banks)
-            for b in range(1 if helped else 0, PAIR_BANKS):
-                if b == 1 and step + 1 < PAIRS:
-                    quantise(step + 1)
-                add_bias_on_vector(step, b, banks)
-                store(step, b)
-                if step == 0 and b == 1:
-                    shape(2)
-                    find_slopes(2, BLOCKS)
-                if step == 0 and b == 2:
-                    shape(3)
-            if step - 1 >= HELP_FROM:
-                store(step - 1, 0)
-            if step + FORM_AHEAD < PAIRS:
-                for h in range(PAIR):
-                    form_on_scalar_and_gpsimd(PAIR * (step + FORM_AHEAD) + h)
+            ks = multiply(step, 0)
+            vs = multiply(step, 1)
+            last = step == PAIRS - 1
+            for w in range(2):
+                for h in range(SIDES):
+                    add_bias(step, w, h, (ks, vs)[w])
+                    if w == 0 and h == 0 and not last:
+                        quantise(step + 1)
+                    if last:
+                        store(step, w, slice(h, h + 1))
+                if not last:
+                    store(step, w)
             if step + TURN_AHEAD < PAIRS:
-                turn_and_regroup(step + TURN_AHEAD)
-        store(PAIRS - 1, 0)
+                turn(step + TURN_AHEAD)
+            if step + FORM_AHEAD < PAIRS:
+                form(step + FORM_AHEAD)

@@ -56,7 +56,7 @@ def tile_causalfeaturetransformer_pa_kernel(
         z_rstd = keep.tile([P, 1], F32)
         f_rows = keep.tile([P, SEQ], F32)
         f_squared = keep.tile([P, BLOCKS, BATCH], F32)
-        e_stats = keep.tile([P, 6], F32)
+        e_stats = keep.tile([P, BLOCKS, 6], F32)
         e_mv = keep.tile([P, BLOCKS, 2], F32)
         e_squares = keep.tile([P, BLOCKS], F32)
         unused = keep.tile([P, D_EMB], BF16)
@@ -64,6 +64,9 @@ def tile_causalfeaturetransformer_pa_kernel(
         root = keep.tile([P, BLOCKS, 2 * BATCH], F32)
         slope = keep.tile([P, BLOCKS, BATCH], F32)
         be1_all = keep.tile([P, PACK, P], F32)
+        g1_all = keep.tile([P, D_EMB], F32)
+        minus_mean = keep.tile([P, BLOCKS], F32)
+        centred = [keep.tile([P, D_EMB], F32, name="centred%d" % j) for j in range(SIDES, BLOCKS)]
         bias_all = [keep.tile([P, D_OUT], BF16, name="bias_all%d" % w) for w in range(2)]
         w_raw = [keep.tile([P, PACK, D_OUT], BF16, name="w_raw%d" % w) for w in range(2)]
         w_grouped = [
@@ -115,8 +118,10 @@ def tile_causalfeaturetransformer_pa_kernel(
             return bank[:, 0 : BLOCKS * BATCH].rearrange("p (j n) -> p j n", n=BATCH)
 
         def measure_on_vector(j):
-            nc.vector.bn_stats(out=e_stats[:], in_=emb[:, j, :])
-            nc.vector.bn_aggr(out=e_mv[:, j, :], in_=e_stats[:])
+            nc.vector.bn_stats(out=e_stats[:, j, :], in_=emb[:, j, :])
+
+        def finish_on_vector(j):
+            nc.vector.bn_aggr(out=e_mv[:, j, :], in_=e_stats[:, j, :])
 
         def measure_on_scalar(j):
             nc.scalar.activation(
@@ -140,6 +145,20 @@ def tile_causalfeaturetransformer_pa_kernel(
                     op0=ALU.subtract,
                     op1=ALU.mult,
                 )
+
+        def shape_on_gpsimd(j):
+            nc.scalar.activation(out=minus_mean[:, j : j + 1], in_=e_mv[:, j, 0:1], func=ACT.Copy, scale=-1.0)
+            nc.gpsimd.tensor_scalar(
+                out=as_they_lie(centred[j - SIDES][:]),
+                in0=by_word(emb[:, j, :]),
+                scalar1=1.0,
+                scalar2=minus_mean[:, j : j + 1],
+                op0=ALU.mult,
+                op1=ALU.add,
+            )
+            nc.gpsimd.tensor_tensor(
+                out=shaped[:, j, :], in0=centred[j - SIDES][:], in1=g1_all[:], op=ALU.mult
+            )
 
         def find_root(j):
             nc.scalar.activation(
@@ -200,11 +219,12 @@ def tile_causalfeaturetransformer_pa_kernel(
             turned = turned_banks.tile([P, PACK, P], F32, name="turned")
             for t in range(PACK):
                 nc.tensor.matmul(
-                    out=turned[:, t, :], lhsT=be1_all[:, t, :], rhs=ident[:], start=True, stop=False,
+                    out=turned[:, t, :], lhsT=be1_all[:, t, :], rhs=ident[:], start=(t == 0), stop=False,
                     is_transpose=True,
                 )
+            for t in range(PACK):
                 nc.tensor.matmul(
-                    out=turned[:, t, :], lhsT=scaled[c, h][:, t, :], rhs=ident[:], start=False, stop=True,
+                    out=turned[:, t, :], lhsT=scaled[c, h][:, t, :], rhs=ident[:], start=False, stop=(t == PACK - 1),
                     is_transpose=True,
                 )
             nc.scalar.copy(out=x_grouped[c][:, h], in_=turned[:].rearrange("p t r -> p r t"))
@@ -283,14 +303,15 @@ def tile_causalfeaturetransformer_pa_kernel(
         nc.scalar.activation(
             out=z_rstd[rows4, :], in_=z_mv[rows4, 1:2], func=ACT.Abs_reciprocal_sqrt, bias=EPS
         )
-        nc.vector.bn_stats(out=e_stats[:], in_=emb[:, 0, :])
+        measure_on_vector(0)
         nc.vector.tensor_scalar(
             out=f_rows[rows4, 0:D_FEAT], in0=z_rows[rows4, 0:D_FEAT], scalar1=z_mv[rows4, 0:1],
             scalar2=z_rstd[rows4, 0:1], op0=ALU.subtract, op1=ALU.mult,
         )
-        nc.vector.bn_aggr(out=e_mv[:, 0, :], in_=e_stats[:])
+        finish_on_vector(0)
         be1_bank = spread_row(1)
         g1_bank = spread_row(0)
+        be1_bank_too = spread_row(1)
         measure_on_scalar(1)
         turned_f = turn_f()
         regroup_weight(0)
@@ -301,19 +322,21 @@ def tile_causalfeaturetransformer_pa_kernel(
         find_root(1)
         nc.scalar.copy(
             out=be1_all[:].rearrange("q (u e) p -> q u e p", u=2),
-            in_=be1_bank[:].rearrange("q (u p e) -> q u e p", u=2, e=2),
+            in_=be1_bank_too[:].rearrange("q (u p e) -> q u e p", u=2, e=2),
         )
         shape(1, g1_bank)
-        measure_on_vector(2)
         find_slopes(0, 2, turned_f)
         form(0)
         form(1)
+        for j in range(SIDES, BLOCKS):
+            measure_on_vector(j)
+        for j in range(SIDES, BLOCKS):
+            finish_on_vector(j)
         turn(0)
-        find_root(2)
-        measure_on_vector(3)
-        shape(2, g1_bank)
-        shape(3, g1_bank)
-        find_root(3)
+        nc.scalar.copy(out=g1_all[:], in_=g1_bank[:])
+        for j in range(SIDES, BLOCKS):
+            find_root(j)
+            shape_on_gpsimd(j)
         turn(1)
         quantise_weight(0)
         quantise(0)
@@ -324,14 +347,15 @@ def tile_causalfeaturetransformer_pa_kernel(
             ks = multiply(step, 0)
             vs = multiply(step, 1)
             last = step == PAIRS - 1
+            one_by_one = last or step == 0
             for w in range(2):
                 for h in range(SIDES):
                     add_bias(step, w, h, (ks, vs)[w])
                     if w == 0 and h == 0 and not last:
                         quantise(step + 1)
-                    if last:
+                    if one_by_one:
                         store(step, w, slice(h, h + 1))
-                if not last:
+                if not one_by_one:
                     store(step, w)
             if step + TURN_AHEAD < PAIRS:
                 turn(step + TURN_AHEAD)

@@ -108,6 +108,10 @@ def tile_causalfeaturetransformer_pa_kernel(
             )
             return bank
 
+        def keep_busy(times):
+            for i in range(times):
+                nc.tensor.matmul(out=spare_bank[:], lhsT=ident_bf[:], rhs=rows[:], start=True, stop=True)
+
         def turn_f():
             bank = acc_banks.tile([P, D_EMB], F32, name="acc")
             for j in range(BLOCKS):
@@ -314,6 +318,8 @@ def tile_causalfeaturetransformer_pa_kernel(
         be1_bank_too = spread_row(1)
         measure_on_scalar(1)
         turned_f = turn_f()
+        spare_bank = acc_banks.tile([P, D_EMB], F32, name="acc")
+        keep_busy(2)
         regroup_weight(0)
         regroup_weight(1)
         shape(0, g1_bank)
@@ -337,7 +343,9 @@ def tile_causalfeaturetransformer_pa_kernel(
         for j in range(SIDES, BLOCKS):
             find_root(j)
             shape_on_gpsimd(j)
+        keep_busy(2)
         turn(1)
+        keep_busy(2)
         quantise_weight(0)
         quantise(0)
         quantise_weight(1)

@@ -319,7 +319,7 @@ def tile_causalfeaturetransformer_pa_kernel(
         measure_on_scalar(1)
         turned_f = turn_f()
         spare_bank = acc_banks.tile([P, D_EMB], F32, name="acc")
-        keep_busy(2)
+        keep_busy(3)
         regroup_weight(0)
         regroup_weight(1)
         shape(0, g1_bank)
@@ -344,8 +344,9 @@ def tile_causalfeaturetransformer_pa_kernel(
             find_root(j)
             shape_on_gpsimd(j)
         keep_busy(2)
-        turn(1)
+        turn_and_add(1, 0)
         keep_busy(2)
+        turn_and_add(1, 1)
         quantise_weight(0)
         quantise(0)
         quantise_weight(1)

from contextlib import ExitStack

import concourse.mybir as mybir
from concourse.masks import make_identity

F32 = mybir.dt.float32
BF16 = mybir.dt.bfloat16
U32 = mybir.dt.uint32
U8 = mybir.dt.uint8
I32 = mybir.dt.int32
FP8X4 = mybir.dt.float8_e4m3fn_x4
ALU = mybir.AluOpType
ACT = mybir.ActivationFunctionType

P = 128
PACK = 4
BATCH = 4
D_FEAT = 511
SEQ = D_FEAT + 1
D_EMB = 512
D_OUT = 512
EPS = 1e-5
HALF = SEQ // 2
SIDES = 2
BLOCKS = 2 * SIDES
PAIRS = 2 * BATCH

TURN_AHEAD = 2
FORM_AHEAD = 3
VECTOR_PAIRS = 1

FLOPS = 2 * BATCH * SEQ * D_EMB * 2 * D_OUT


def tile_causalfeaturetransformer_pa_kernel(
    tc, Z, feat_emb, label_token, g1, be1, wk, bk, wv, bv, out_0, out_1
):
    nc = tc.nc
    weights = (wk, wv)
    outs = (out_0, out_1)

    with ExitStack() as ctx:
        keep = ctx.enter_context(tc.tile_pool(name="keep", bufs=1))
        turned_banks = ctx.enter_context(tc.psum_pool(name="turned_banks", bufs=2))
        acc_banks = ctx.enter_context(tc.psum_pool(name="acc_banks", bufs=6))
        ctx.enter_context(tc.manual_schedule())

        ident = keep.tile([P, P], F32)
        ident_bf = keep.tile([P, P], BF16)
        warm = keep.tile([P, 1], F32)
        z_rows = keep.tile([P, SEQ], BF16)
        rows = keep.tile([P, D_EMB], BF16)
        emb = keep.tile([P, BLOCKS, D_EMB], BF16)
        z_stats = keep.tile([P, 6], F32)
        z_mv = keep.tile([P, 2], F32)
        z_rstd = keep.tile([P, 1], F32)
        f_rows = keep.tile([P, SEQ], F32)
        f_squared = keep.tile([P, BLOCKS, BATCH], F32)
        e_stats = keep.tile([P, BLOCKS, 6], F32)
        e_mv = keep.tile([P, BLOCKS, 2], F32)
        e_squares = keep.tile([P, BLOCKS], F32)
        unused = keep.tile([P, D_EMB], BF16)
        shaped = keep.tile([P, BLOCKS, D_EMB], F32)
        root = keep.tile([P, BLOCKS, 2 * BATCH], F32)
        slope = keep.tile([P, BLOCKS, BATCH], F32)
        be1_all = keep.tile([P, PACK, P], F32)
        g1_all = keep.tile([P, D_EMB], F32)
        minus_mean = keep.tile([P, BLOCKS], F32)
        centred = [keep.tile([P, D_EMB], F32, name="centred%d" % j) for j in range(SIDES, BLOCKS)]
        bias_all = [keep.tile([P, D_OUT], BF16, name="bias_all%d" % w) for w in range(2)]
        w_raw = [keep.tile([P, PACK, D_OUT], BF16, name="w_raw%d" % w) for w in range(2)]
        w_grouped = [
            keep.tile([P, D_OUT, PACK], BF16, name="w_grouped%d" % w, align_bytes=64) for w in range(2)
        ]
        w_codes = [keep.tile([P, D_OUT], U32, name="w_codes%d" % w, align_bytes=64) for w in range(2)]
        w_scales = [keep.tile([P, D_OUT], U8, name="w_scales%d" % w, align_bytes=64) for w in range(2)]
        xn = {
            (c, h): keep.tile([P, D_EMB], BF16, name="xn%d_%d" % (c, h))
            for c in range(VECTOR_PAIRS) for h in range(SIDES)
        }
        scaled = {
            (c, h): keep.tile([P, PACK, P], F32, name="scaled%d_%d" % (c, h))
            for c in range(VECTOR_PAIRS, PAIRS) for h in range(SIDES)
        }
        x_grouped = [
            keep.tile([P, SIDES, P, PACK], BF16, name="x_grouped%d" % c, align_bytes=64) for c in range(PAIRS)
        ]
        x_codes = [keep.tile([P, SIDES * P], U32, name="x_codes%d" % c, align_bytes=64) for c in range(PAIRS)]
        x_scales = [keep.tile([P, SIDES * P], U8, name="x_scales%d" % c, align_bytes=64) for c in range(PAIRS)]
        result = [
            [keep.tile([P, SIDES, D_OUT], F32, name="result%d_%d" % (c, w)) for w in range(2)] for c in range(PAIRS)
        ]

        def by_word(x):
            return x.rearrange("q (p u e) -> q u p e", u=2, e=2)

        def as_they_lie(x):
            return x.rearrange("q (u p e) -> q u p e", u=2, e=2)

        def spread_row(r):
            bank = acc_banks.tile([P, D_EMB], F32, name="acc")
            nc.tensor.matmul(
                out=as_they_lie(bank[:]),
                lhsT=ident_bf[:, r : r + 1].to_broadcast([P, P]),
                rhs=by_word(rows[:]),
                start=True,
                stop=True,
            )
            return bank

        def keep_busy(times):
            for i in range(times):
                nc.tensor.matmul(out=spare_bank[:], lhsT=ident_bf[:], rhs=rows[:], start=True, stop=True)

        def turn_f():
            bank = acc_banks.tile([P, D_EMB], F32, name="acc")
            for j in range(BLOCKS):
                half, h = divmod(j, SIDES)
                nc.tensor.transpose(
                    bank[:, BATCH * j : BATCH * j + P], f_rows[:, half * HALF + h : (half + 1) * HALF : SIDES], ident[:]
                )
            return bank[:, 0 : BLOCKS * BATCH].rearrange("p (j n) -> p j n", n=BATCH)

        def measure_on_vector(j):
            nc.vector.bn_stats(out=e_stats[:, j, :], in_=emb[:, j, :])

        def finish_on_vector(j):
            nc.vector.bn_aggr(out=e_mv[:, j, :], in_=e_stats[:, j, :])

        def measure_on_scalar(j):
            nc.scalar.activation(
                out=unused[:], in_=emb[:, j, :], func=ACT.Copy, scale=1.0 / D_EMB, accum_out=e_mv[:, j, 0:1]
            )
            nc.scalar.activation(
                out=unused[:], in_=emb[:, j, :], func=ACT.Square, scale=-1.0, bias=e_mv[:, j, 0:1],
                accum_out=e_squares[:, j : j + 1],
            )
            nc.scalar.activation(
                out=e_mv[:, j, 1:2], in_=e_squares[:, j : j + 1], func=ACT.Copy, scale=1.0 / D_EMB
            )

        def shape(j, gain):
            for u in range(2):
                nc.vector.scalar_tensor_tensor(
                    out=as_they_lie(shaped[:, j, :])[:, u],
                    in0=by_word(emb[:, j, :])[:, u],
                    scalar=e_mv[:, j, 0:1],
                    in1=as_they_lie(gain[:])[:, u],
                    op0=ALU.subtract,
                    op1=ALU.mult,
                )

        def shape_on_gpsimd(j):
            nc.scalar.activation(out=minus_mean[:, j : j + 1], in_=e_mv[:, j, 0:1], func=ACT.Copy, scale=-1.0)
            nc.gpsimd.tensor_scalar(
                out=as_they_lie(centred[j - SIDES][:]),
                in0=by_word(emb[:, j, :]),
                scalar1=1.0,
                scalar2=minus_mean[:, j : j + 1],
                op0=ALU.mult,
                op1=ALU.add,
            )
            nc.gpsimd.tensor_tensor(
                out=shaped[:, j, :], in0=centred[j - SIDES][:], in1=g1_all[:], op=ALU.mult
            )

        def find_root(j):
            nc.scalar.activation(
                out=root[:, j, 0:BATCH], in_=f_squared[:, j, :], func=ACT.Abs_reciprocal_sqrt,
                scale=e_mv[:, j, 1:2], bias=EPS,
            )

        def find_slopes(first, end, f_of):
            nc.vector.tensor_mul(
                out=slope[:, first:end, :], in0=f_of[:, first:end, :], in1=root[:, first:end, 0:BATCH]
            )

        def regroup_weight(w):
            nc.gpsimd.tensor_scalar(
                out=w_grouped[w][:],
                in0=w_raw[w][:].rearrange("p t n -> p n t"),
                scalar1=1.0,
                scalar2=0.0,
                op0=ALU.mult,
                op1=ALU.add,
            )

        def quantise_weight(w):
            nc.vector.quantize_mx(
                out=w_codes[w][:].bitcast(FP8X4),
                scales=w_scales[w][:],
                in_=w_grouped[w][:].rearrange("p n t -> p (n t)"),
            )

        def form(c):
            half, n = divmod(c, BATCH)
            for h in range(SIDES):
                j = SIDES * half + h
                if c < VECTOR_PAIRS:
                    nc.vector.scalar_tensor_tensor(
                        out=xn[c, h][:], in0=shaped[:, j, :], scalar=slope[:, j, n : n + 1], in1=be1_bank[:],
                        op0=ALU.mult, op1=ALU.add,
                    )
                    continue
                out = scaled[c, h][:].rearrange("q (u e) p -> q u e p", u=2)
                in_ = shaped[:, j, :].rearrange("q (u p e) -> q u e p", u=2, e=2)
                nc.scalar.activation(out=out, in_=in_, func=ACT.Copy, scale=slope[:, j, n : n + 1])

        def turn_words(c):
            turned = turned_banks.tile([P, SIDES, 2, P], F32, name="turned")
            for h in range(SIDES):
                words = xn[c, h][:].bitcast(F32)
                for u in range(2):
                    nc.tensor.transpose(turned[:, h, u, :], words[:, u * P : (u + 1) * P], ident[:])
            nc.scalar.copy(
                out=x_grouped[c][:].rearrange("p h r t -> p (h r t)").bitcast(F32).rearrange(
                    "p (h r u) -> p h r u", h=SIDES, u=2
                ),
                in_=turned[:].rearrange("p h u r -> p h r u"),
            )

        def turn_and_add(c, h):
            turned = turned_banks.tile([P, PACK, P], F32, name="turned")
            for t in range(PACK):
                nc.tensor.matmul(
                    out=turned[:, t, :], lhsT=be1_all[:, t, :], rhs=ident[:], start=(t == 0), stop=False,
                    is_transpose=True,
                )
            for t in range(PACK):
                nc.tensor.matmul(
                    out=turned[:, t, :], lhsT=scaled[c, h][:, t, :], rhs=ident[:], start=False, stop=(t == PACK - 1),
                    is_transpose=True,
                )
            nc.scalar.copy(out=x_grouped[c][:, h], in_=turned[:].rearrange("p t r -> p r t"))

        def turn(c):
            if c < VECTOR_PAIRS:
                turn_words(c)
            else:
                for h in range(SIDES):
                    turn_and_add(c, h)

        def quantise(c):
            nc.vector.quantize_mx(
                out=x_codes[c][:].bitcast(FP8X4),
                scales=x_scales[c][:],
                in_=x_grouped[c][:].rearrange("p h r t -> p (h r t)"),
            )

        def multiply(c, w):
            banks = []
            for h in range(SIDES):
                tokens = slice(h * P, (h + 1) * P)
                acc = acc_banks.tile([P, D_OUT], F32, name="acc")
                nc.tensor.matmul_mx(
                    out=acc[:],
                    lhsT=x_codes[c][:, tokens].bitcast(FP8X4),
                    lhsT_scale=x_scales[c][:, tokens],
                    rhs=w_codes[w][:].bitcast(FP8X4),
                    rhs_scale=w_scales[w][:],
                    start=True,
                    stop=True,
                )
                banks.append(acc)
            return banks

        def add_bias(c, w, h, banks):
            nc.vector.tensor_add(out=result[c][w][:, h, :], in0=banks[h][:], in1=bias_all[w][:])

        def store(c, w, sides=slice(0, SIDES)):
            half, n = divmod(c, BATCH)
            out = outs[w][n, half * HALF : (half + 1) * HALF, :].rearrange("(p h) k -> p h k", h=SIDES)
            nc.sync.dma_start(out=out[:, sides, :], in_=result[c][w][:, sides, :])

        def load_row(r, vector):
            nc.sync.dma_start(out=rows[r : r + 1, :], in_=vector.rearrange("(a k) -> a k", a=1))

        def load_weight(w):
            nc.sync.dma_start(out=w_raw[w][:], in_=weights[w].rearrange("(p t) n -> p t n", p=P))

        nc.gpsimd.memset(rows[:].bitcast(I32), 0)
        nc.gpsimd.memset(warm[:], 1.0)
        nc.sync.dma_start(out=z_rows[0:BATCH, 0:D_FEAT], in_=Z)
        nc.sync.dma_start(
            out=emb[:, 0:SIDES, :], in_=feat_emb[0:HALF, :].rearrange("(p h) k -> p h k", h=SIDES)
        )
        load_row(0, g1)
        load_row(1, be1)
        load_weight(0)
        nc.sync.dma_start(out=emb[:, SIDES, :], in_=feat_emb[HALF:D_FEAT:SIDES, :])
        load_weight(1)
        nc.sync.dma_start(out=emb[0:112, SIDES + 1, :], in_=feat_emb[HALF + 1 : HALF + 1 + 2 * 112 : SIDES, :])
        nc.sync.dma_start(out=emb[112:127, SIDES + 1, :], in_=feat_emb[HALF + 1 + 2 * 112 : D_FEAT : SIDES, :])
        nc.sync.dma_start(out=emb[127:128, SIDES + 1, :], in_=label_token.rearrange("a b k -> (a b) k"))
        nc.sync.dma_start(out=bias_all[0][:], in_=bk.partition_broadcast(P))
        nc.sync.dma_start(out=bias_all[1][:], in_=bv.partition_broadcast(P))

        make_identity(nc, ident_bf[:])
        nc.gpsimd.memset(f_rows[:], 0.0)
        make_identity(nc, ident[:])
        nc.scalar.activation(out=warm[:], in_=warm[:], func=ACT.Abs_reciprocal_sqrt)

        rows4 = slice(0, BATCH)
        nc.vector.memset(f_rows[rows4, D_FEAT:SEQ], 1.0)
        nc.vector.bn_stats(out=z_stats[rows4, :], in_=z_rows[rows4, 0:D_FEAT])
        nc.vector.bn_aggr(out=z_mv[rows4, :], in_=z_stats[rows4, :])
        nc.scalar.activation(
            out=z_rstd[rows4, :], in_=z_mv[rows4, 1:2], func=ACT.Abs_reciprocal_sqrt, bias=EPS
        )
        measure_on_vector(0)
        nc.vector.tensor_scalar(
            out=f_rows[rows4, 0:D_FEAT], in0=z_rows[rows4, 0:D_FEAT], scalar1=z_mv[rows4, 0:1],
            scalar2=z_rstd[rows4, 0:1], op0=ALU.subtract, op1=ALU.mult,
        )
        finish_on_vector(0)
        be1_bank = spread_row(1)
        g1_bank = spread_row(0)
        be1_bank_too = spread_row(1)
        measure_on_scalar(1)
        turned_f = turn_f()
        spare_bank = acc_banks.tile([P, D_EMB], F32, name="acc")
        keep_busy(3)
        regroup_weight(0)
        regroup_weight(1)
        shape(0, g1_bank)
        nc.scalar.activation(out=f_squared[:], in_=turned_f, func=ACT.Square)
        find_root(0)
        find_root(1)
        nc.scalar.copy(
            out=be1_all[:].rearrange("q (u e) p -> q u e p", u=2),
            in_=be1_bank_too[:].rearrange("q (u p e) -> q u e p", u=2, e=2),
        )
        shape(1, g1_bank)
        find_slopes(0, 2, turned_f)
        form(0)
        form(1)
        for j in range(SIDES, BLOCKS):
            measure_on_vector(j)
        for j in range(SIDES, BLOCKS):
            finish_on_vector(j)
        turn(0)
        nc.scalar.copy(out=g1_all[:], in_=g1_bank[:])
        for j in range(SIDES, BLOCKS):
            find_root(j)
            shape_on_gpsimd(j)
        keep_busy(2)
        turn_and_add(1, 0)
        keep_busy(2)
        turn_and_add(1, 1)
        quantise_weight(0)
        quantise(0)
        quantise_weight(1)
        find_slopes(2, 4, turned_f)
        form(2)
        for step in range(PAIRS):
            ks = multiply(step, 0)
            vs = multiply(step, 1)
            last = step == PAIRS - 1
            one_by_one = last or step == 0
            for w in range(2):
                for h in range(SIDES):
                    add_bias(step, w, h, (ks, vs)[w])
                    if w == 0 and h == 0 and not last:
                        quantise(step + 1)
                    if one_by_one:
                        store(step, w, slice(h, h + 1))
                if not one_by_one:
                    store(step, w)
            if step + TURN_AHEAD < PAIRS:
                turn(step + TURN_AHEAD)
            if step + FORM_AHEAD < PAIRS:
                form(step + FORM_AHEAD)
